import numpy as np
import ml_dtypes


def mxq(x, axis, fmt="e4m3"):
    dtype, down = {"e4m3": (ml_dtypes.float8_e4m3fn, 7), "e5m2": (ml_dtypes.float8_e5m2, 14)}[fmt]
    v = np.moveaxis(np.asarray(x, np.float32).astype(ml_dtypes.bfloat16).astype(np.float64), axis, -1)
    blocks = v.reshape(v.shape[:-1] + (-1, 32))
    amax = np.abs(blocks).max(-1, keepdims=True)
    byte = np.maximum(np.where(amax > 0, np.frexp(amax)[1] - 1 + 127, 0) - down, 1)
    scale = np.exp2(byte - 127.0)
    codes = (blocks / scale).astype(np.float32).astype(dtype).astype(np.float64)
    return np.moveaxis((codes * scale).reshape(v.shape), -1, axis)


WIDE = False


def mx_kscale(k):
    if not WIDE:
        return np.ones(k)
    levels = np.array([10, -10, 5, -5, 0])
    a = np.random.permutation(np.resize(levels, k // 512 * 4)).reshape(k // 512, 4)
    idx = np.arange(k)
    return np.exp2(a[idx // 512, idx % 128 // 32])


BF16 = ml_dtypes.bfloat16


def bf(x):
    return np.asarray(x, np.float32).astype(BF16)


def f64(x):
    return np.asarray(x).astype(np.float64)


H, D_CONTENT, D_POS, D_K, D_V, B, L = 16, 512, 128, 128, 128, 8, 512
D_MODEL = D_CONTENT + D_POS
T = B * L
DV1 = D_V // 2
KP = H * DV1
EPS = 1e-3


def setup_inputs():
    s1, s2 = mx_kscale(KP), mx_kscale(KP)
    sc = np.concatenate([s1.reshape(H, DV1), s2.reshape(H, DV1)], axis=1)
    return {
        "attn_out": bf(np.random.standard_normal((H, B, L, D_V)) * 0.4 * sc[:, None, None, :]),
        "inp": bf(np.random.standard_normal((T, D_MODEL)) * 0.05 + np.random.standard_normal((T, 1)) * 0.03),
        "w_proj1": bf(np.random.standard_normal((KP, D_CONTENT)) * 0.1 / np.sqrt(KP) / s1[:, None]),
        "w_proj2": bf(np.random.standard_normal((KP, D_POS)) * 0.1 / np.sqrt(KP) / s2[:, None]),
        "ln_a": bf(1.0 + 0.1 * np.random.standard_normal(D_MODEL)),
        "ln_b": bf(0.1 * np.random.standard_normal(D_MODEL)),
    }


def reference(attn_out, inp, w_proj1, w_proj2, ln_a, ln_b):
    o = f64(attn_out).reshape(H, T, D_V).transpose(1, 0, 2)
    o1 = o[:, :, :DV1].reshape(T, KP)
    o2 = o[:, :, DV1:].reshape(T, KP)
    y1 = mxq(o1, 1, "e4m3") @ mxq(f64(w_proj1), 0, "e4m3")
    y2 = mxq(o2, 1, "e4m3") @ mxq(f64(w_proj2), 0, "e4m3")
    z = np.concatenate([y1, y2], -1) + f64(inp)
    mu = np.mean(z, axis=-1, keepdims=True)
    sigma = np.std(z, axis=-1, keepdims=True, ddof=1)
    ln = (z - mu) / (sigma + EPS)
    return ln * f64(ln_a) + f64(ln_b)

@@ -1,0 +1,239 @@
+from contextlib import ExitStack
+
+import concourse.mybir as mybir
+from concourse.masks import make_identity
+
+BF16 = mybir.dt.bfloat16
+F32 = mybir.dt.float32
+U32 = mybir.dt.uint32
+U8 = mybir.dt.uint8
+FP8X4 = mybir.dt.float8_e4m3fn_x4
+ALU = mybir.AluOpType
+ACT = mybir.ActivationFunctionType
+
+P = 128
+PACK = 4
+HEADS = 16
+TOKENS = 4096
+D_V = 128
+HALF = 64
+D_CONTENT = 512
+D_POS = 128
+D_MODEL = D_CONTENT + D_POS
+EPS = 1e-3
+
+N_TILES = TOKENS // P
+HEAD_SETS = 2
+PARITIES = 2
+SLABS = 8
+ROUND = 2
+N_ROUNDS = N_TILES // ROUND
+CHUNK = 4
+N_CHUNKS = N_TILES // CHUNK
+CHUNKS_AHEAD = 2
+
+FLOPS = 2 * TOKENS * (HEADS * HALF) * D_MODEL
+
+
+def tile_multiheadattention_pa_t_kernel(tc, attn_out, inp, w_proj1, w_proj2, ln_a, ln_b, out):
+    nc = tc.nc
+    x_view = attn_out.flatten_outer_dims().rearrange(
+        "(g p s k) f -> g p s k f", g=HEAD_SETS, p=P, s=SLABS
+    )
+    inp_view = inp.rearrange("(m k) c -> m k c", k=N_TILES)
+    out_view = out.rearrange("(m k) c -> m k c", k=N_TILES)
+
+    with ExitStack() as ctx:
+        const = ctx.enter_context(tc.tile_pool(name="const", bufs=1))
+        xin = ctx.enter_context(tc.tile_pool(name="xin", bufs=3))
+        resin = ctx.enter_context(tc.tile_pool(name="resin", bufs=4))
+        grouped = ctx.enter_context(tc.tile_pool(name="grouped", bufs=4))
+        packed = ctx.enter_context(tc.tile_pool(name="packed", bufs=6))
+        work = ctx.enter_context(tc.tile_pool(name="work", bufs=4))
+        stats = ctx.enter_context(tc.tile_pool(name="stats", bufs=8))
+        result = ctx.enter_context(tc.tile_pool(name="result", bufs=3))
+        t_psum = ctx.enter_context(tc.psum_pool(name="t_psum", bufs=4))
+        y_psum = ctx.enter_context(tc.psum_pool(name="y_psum", bufs=2))
+
+        x_tiles = {}
+        res_tiles = {}
+
+        def load_chunk(c):
+            k0 = c * CHUNK
+            x = xin.tile([P, HEAD_SETS, SLABS, CHUNK, D_V], BF16)
+            for g in range(HEAD_SETS):
+                nc.sync.dma_start(out=x[:, g], in_=x_view[g, :, :, k0 : k0 + CHUNK, :])
+            res = resin.tile([P, CHUNK, D_MODEL], BF16)
+            nc.sync.dma_start(out=res[:], in_=inp_view[:, k0 : k0 + CHUNK, :])
+            x_tiles[c] = x
+            res_tiles[c] = res
+
+        w1_grouped = const.tile([P, 4, D_CONTENT, PACK], BF16, align_bytes=64)
+        w2_grouped = const.tile([P, 4, D_POS, PACK], BF16, align_bytes=64)
+        nc.vector.memset(w1_grouped[HALF:P], 0.0)
+        nc.vector.memset(w2_grouped[0:HALF], 0.0)
+
+        ident = const.tile([P, P], BF16)
+        make_identity(nc, ident[:])
+        perm = const.tile([P, P], BF16)
+        nc.vector.tensor_copy(
+            out=perm[:].rearrange("p (c t) -> p c t", t=PACK),
+            in_=ident[:].rearrange("p (t c) -> p c t", t=PACK),
+        )
+
+        load_chunk(0)
+
+        w1_raw = const.tile([P, HEADS, D_CONTENT], BF16)
+        w2_raw = const.tile([P, HEADS, D_POS], BF16)
+        nc.sync.dma_start(out=w1_raw[0:HALF], in_=w_proj1.rearrange("(h j) n -> j h n", j=HALF))
+        nc.sync.dma_start(out=w2_raw[HALF:P], in_=w_proj2.rearrange("(h j) n -> j h n", j=HALF))
+
+        load_chunk(1)
+
+        gain = const.tile([P, D_MODEL], BF16)
+        shift = const.tile([P, D_MODEL], BF16)
+        nc.sync.dma_start(out=gain[:], in_=ln_a.partition_broadcast(P))
+        nc.sync.dma_start(out=shift[:], in_=ln_b.partition_broadcast(P))
+
+        w1_codes = const.tile([P, 4, D_CONTENT], U32, align_bytes=64)
+        w1_scales = const.tile([P, 4, D_CONTENT], U8, align_bytes=64)
+        w2_codes = const.tile([P, 4, D_POS], U32, align_bytes=64)
+        w2_scales = const.tile([P, 4, D_POS], U8, align_bytes=64)
+        w1_by_set = w1_raw[0:HALF].rearrange("p (g t r) n -> p g r n t", g=HEAD_SETS, t=PACK, r=PARITIES)
+        w2_by_set = w2_raw[HALF:P].rearrange("p (g t r) n -> p g r n t", g=HEAD_SETS, t=PACK, r=PARITIES)
+        for g in range(HEAD_SETS):
+            for r in range(PARITIES):
+                nc.vector.tensor_copy(out=w1_grouped[0:HALF, 2 * g + r], in_=w1_by_set[:, g, r])
+                nc.vector.tensor_copy(out=w2_grouped[HALF:P, 2 * g + r], in_=w2_by_set[:, g, r])
+        for q in range(4):
+            nc.vector.quantize_mx(
+                out=w1_codes[:, q, :].bitcast(FP8X4),
+                scales=w1_scales[:, q, :],
+                in_=w1_grouped[:, q].rearrange("p n t -> p (n t)"),
+            )
+        nc.vector.quantize_mx(
+            out=w2_codes[:].rearrange("p q n -> p (q n)").bitcast(FP8X4),
+            scales=w2_scales[:].rearrange("p q n -> p (q n)"),
+            in_=w2_grouped[:].rearrange("p q n t -> p (q n t)"),
+        )
+
+        xg_tiles = {}
+        code_tiles = {}
+        y_tiles = {}
+        z_tiles = {}
+        stat_tiles = {}
+        u_tiles = {}
+
+        def tiles_of(rnd):
+            return range(rnd * ROUND, (rnd + 1) * ROUND)
+
+        def transpose_round(rnd):
+            for k in tiles_of(rnd):
+                x = x_tiles[k // CHUNK]
+                xg = grouped.tile([P, HEAD_SETS, SLABS * P], BF16, align_bytes=64)
+                for g in range(HEAD_SETS):
+                    bank = t_psum.tile([P, P // PACK, SLABS, PACK], BF16)
+                    for s in range(SLABS):
+                        nc.tensor.transpose(bank[:, :, s, :], x[:, g, s, k % CHUNK, :], perm[:])
+                    nc.scalar.copy(out=xg[:, g, :], in_=bank[:].rearrange("p c s t -> p (c s t)"))
+                xg_tiles[k] = xg
+
+        def quantise_round(rnd):
+            for k in tiles_of(rnd):
+                codes = packed.tile([P, 4, P], U32, align_bytes=64)
+                scales = packed.tile([P, 4, P], U8, align_bytes=64)
+                nc.vector.quantize_mx(
+                    out=codes[:].rearrange("p q m -> p (q m)").bitcast(FP8X4),
+                    scales=scales[:].rearrange("p q m -> p (q m)"),
+                    in_=xg_tiles[k][:].rearrange("p g w -> p (g w)"),
+                )
+                code_tiles[k] = (codes, scales)
+
+        def multiply_round(rnd):
+            for k in tiles_of(rnd):
+                codes, scales = code_tiles[k]
+                y1 = y_psum.tile([P, D_CONTENT], F32)
+                y2 = y_psum.tile([P, D_POS], F32)
+                for q in range(4):
+                    nc.tensor.matmul_mx(
+                        out=y1[:],
+                        lhsT=codes[:, q, :].bitcast(FP8X4),
+                        lhsT_scale=scales[:, q, :],
+                        rhs=w1_codes[:, q, :].bitcast(FP8X4),
+                        rhs_scale=w1_scales[:, q, :],
+                        start=(q == 0),
+                        stop=(q == 3),
+                    )
+                for q in range(4):
+                    nc.tensor.matmul_mx(
+                        out=y2[:],
+                        lhsT=codes[:, q, :].bitcast(FP8X4),
+                        lhsT_scale=scales[:, q, :],
+                        rhs=w2_codes[:, q, :].bitcast(FP8X4),
+                        rhs_scale=w2_scales[:, q, :],
+                        start=(q == 0),
+                        stop=(q == 3),
+                    )
+                y_tiles[k] = (y1, y2)
+
+        def residual_round(rnd):
+            for k in tiles_of(rnd):
+                y1, y2 = y_tiles[k]
+                res = res_tiles[k // CHUNK]
+                z = work.tile([P, D_MODEL], F32)
+                sums = stats.tile([P, 2], F32)
+                nc.vector.scalar_tensor_tensor(
+                    out=z[:, 0:D_CONTENT], in0=y1[:], scalar=1.0, in1=res[:, k % CHUNK, 0:D_CONTENT],
+                    op0=ALU.mult, op1=ALU.add, accum_out=sums[:, 0:1],
+                )
+                nc.vector.scalar_tensor_tensor(
+                    out=z[:, D_CONTENT:D_MODEL], in0=y2[:], scalar=1.0, in1=res[:, k % CHUNK, D_CONTENT:D_MODEL],
+                    op0=ALU.mult, op1=ALU.add, accum_out=sums[:, 1:2],
+                )
+                neg_mean = stats.tile([P, 1], F32)
+                nc.vector.tensor_scalar(
+                    out=neg_mean[:], in0=sums[:, 0:1], scalar1=sums[:, 1:2], scalar2=-1.0 / D_MODEL,
+                    op0=ALU.add, op1=ALU.mult,
+                )
+                squares = work.tile([P, D_MODEL], F32)
+                sum_sq = stats.tile([P, 1], F32)
+                nc.scalar.activation(
+                    out=squares[:], in_=z[:], func=ACT.Square, bias=neg_mean[:, 0:1], scale=1.0,
+                    accum_out=sum_sq[:, 0:1],
+                )
+                sigma = stats.tile([P, 1], F32)
+                nc.scalar.activation(out=sigma[:], in_=sum_sq[:], func=ACT.Sqrt, scale=1.0 / (D_MODEL - 1))
+                u = work.tile([P, D_MODEL], F32)
+                nc.vector.scalar_tensor_tensor(
+                    out=u[:], in0=z[:], scalar=neg_mean[:, 0:1], in1=gain[:], op0=ALU.add, op1=ALU.mult,
+                )
+                u_tiles[k] = u
+                stat_tiles[k] = sigma
+
+        def finish_round(rnd):
+            o = result.tile([P, ROUND, D_MODEL], F32)
+            for k in tiles_of(rnd):
+                sigma_eps = stats.tile([P, 1], F32)
+                nc.vector.tensor_scalar_add(out=sigma_eps[:], in0=stat_tiles[k][:], scalar1=EPS)
+                inv = stats.tile([P, 1], F32)
+                nc.vector.reciprocal(out=inv[:], in_=sigma_eps[:])
+                nc.vector.scalar_tensor_tensor(
+                    out=o[:, k % ROUND, :], in0=u_tiles[k][:], scalar=inv[:, 0:1], in1=shift[:],
+                    op0=ALU.mult, op1=ALU.add,
+                )
+            k0 = rnd * ROUND
+            nc.sync.dma_start(out=out_view[:, k0 : k0 + ROUND, :], in_=o[:])
+
+        for step in range(N_ROUNDS + 3):
+            if step % 2 == 0 and step // 2 + CHUNKS_AHEAD < N_CHUNKS:
+                load_chunk(step // 2 + CHUNKS_AHEAD)
+            if step < N_ROUNDS:
+                transpose_round(step)
+            if 0 <= step - 2 < N_ROUNDS:
+                residual_round(step - 2)
+            if step < N_ROUNDS:
+                quantise_round(step)
+            if 0 <= step - 1 < N_ROUNDS:
+                multiply_round(step - 1)
+            if 0 <= step - 3 < N_ROUNDS:
+                finish_round(step - 3)

@@ -25,11 +25,13 @@ EPS = 1e-3
 N_TILES = TOKENS // P
 HEAD_SETS = 2
 PARITIES = 2
+QUADS = HEAD_SETS * PARITIES
 SLABS = 8
 ROUND = 2
 N_ROUNDS = N_TILES // ROUND
 CHUNK = 4
 N_CHUNKS = N_TILES // CHUNK
+ROUNDS_PER_CHUNK = CHUNK // ROUND
 CHUNKS_AHEAD = 2
 
 FLOPS = 2 * TOKENS * (HEADS * HALF) * D_MODEL
@@ -44,34 +46,62 @@ def tile_multiheadattention_pa_t_kernel(tc, attn_out, inp, w_proj1, w_proj2, ln_
     out_view = out.rearrange("(m k) c -> m k c", k=N_TILES)
 
     with ExitStack() as ctx:
+        ctx.enter_context(tc.manual_schedule())
         const = ctx.enter_context(tc.tile_pool(name="const", bufs=1))
         xin = ctx.enter_context(tc.tile_pool(name="xin", bufs=3))
-        resin = ctx.enter_context(tc.tile_pool(name="resin", bufs=4))
-        grouped = ctx.enter_context(tc.tile_pool(name="grouped", bufs=4))
-        packed = ctx.enter_context(tc.tile_pool(name="packed", bufs=6))
-        work = ctx.enter_context(tc.tile_pool(name="work", bufs=4))
+        resin = ctx.enter_context(tc.tile_pool(name="resin", bufs=3))
+        grouped = ctx.enter_context(tc.tile_pool(name="grouped", bufs=6))
+        packed = ctx.enter_context(tc.tile_pool(name="packed", bufs=4))
+        zpool = ctx.enter_context(tc.tile_pool(name="zpool", bufs=4))
+        upool = ctx.enter_context(tc.tile_pool(name="upool", bufs=6))
+        scratch = ctx.enter_context(tc.tile_pool(name="scratch", bufs=2))
         stats = ctx.enter_context(tc.tile_pool(name="stats", bufs=8))
         result = ctx.enter_context(tc.tile_pool(name="result", bufs=3))
         t_psum = ctx.enter_context(tc.psum_pool(name="t_psum", bufs=4))
-        y_psum = ctx.enter_context(tc.psum_pool(name="y_psum", bufs=2))
+        y1_psum = ctx.enter_context(tc.psum_pool(name="y1_psum", bufs=2))
+        y2_psum = ctx.enter_context(tc.psum_pool(name="y2_psum", bufs=1))
+        gain_psum = ctx.enter_context(tc.psum_pool(name="gain_psum", bufs=1))
 
         x_tiles = {}
         res_tiles = {}
 
-        def load_chunk(c):
+        def load_x(c):
             k0 = c * CHUNK
             x = xin.tile([P, HEAD_SETS, SLABS, CHUNK, D_V], BF16)
             for g in range(HEAD_SETS):
                 nc.sync.dma_start(out=x[:, g], in_=x_view[g, :, :, k0 : k0 + CHUNK, :])
+            x_tiles[c] = x
+
+        def load_residual(c):
+            k0 = c * CHUNK
             res = resin.tile([P, CHUNK, D_MODEL], BF16)
             nc.sync.dma_start(out=res[:], in_=inp_view[:, k0 : k0 + CHUNK, :])
-            x_tiles[c] = x
             res_tiles[c] = res
 
-        w1_grouped = const.tile([P, 4, D_CONTENT, PACK], BF16, align_bytes=64)
-        w2_grouped = const.tile([P, 4, D_POS, PACK], BF16, align_bytes=64)
+        ln_rows = const.tile([P, 2, D_MODEL], BF16)
+        nc.vector.memset(ln_rows[:], 0.0)
+        nc.sync.dma_start(out=ln_rows[0:1, 0, :], in_=ln_a.unsqueeze(0))
+        nc.sync.dma_start(out=ln_rows[0:1, 1, :], in_=ln_b.unsqueeze(0))
+        w1_raw = const.tile([P, HEAD_SETS, HEADS // HEAD_SETS, D_CONTENT], BF16)
+        w2_raw = const.tile([P, HEADS, D_POS], BF16)
+        nc.sync.dma_start(out=w2_raw[HALF:P], in_=w_proj2.rearrange("(h j) n -> j h n", j=HALF))
+        load_x(0)
+        w1_view = w_proj1.rearrange("(g h j) n -> g j h n", g=HEAD_SETS, j=HALF)
+        for g in range(HEAD_SETS):
+            nc.sync.dma_start(out=w1_raw[0:HALF, g], in_=w1_view[g])
+        load_x(1)
+
+        ones = const.tile([P, P], BF16)
+        nc.vector.memset(ones[:], 1.0)
+        w1_grouped = const.tile([P, QUADS, D_CONTENT, PACK], BF16, align_bytes=64)
+        w2_grouped = const.tile([P, QUADS, D_POS, PACK], BF16, align_bytes=64)
         nc.vector.memset(w1_grouped[HALF:P], 0.0)
         nc.vector.memset(w2_grouped[0:HALF], 0.0)
+
+        warm = const.tile([P, 1], F32)
+        nc.vector.memset(warm[:], 1.0)
+        warm_out = const.tile([P, 1], F32)
+        nc.scalar.activation(out=warm_out[:], in_=warm[:], func=ACT.Sqrt)
 
         ident = const.tile([P, P], BF16)
         make_identity(nc, ident[:])
@@ -81,48 +111,56 @@ def tile_multiheadattention_pa_t_kernel(tc, attn_out, inp, w_proj1, w_proj2, ln_
             in_=ident[:].rearrange("p (t c) -> p c t", t=PACK),
         )
 
-        load_chunk(0)
+        gain_head = gain_psum.tile([P, D_CONTENT], F32)
+        nc.tensor.matmul(out=gain_head[:], lhsT=ones[:], rhs=ln_rows[:, 0, 0:D_CONTENT], start=True, stop=True)
+        shift_bank = y1_psum.tile([P, D_CONTENT], F32, tag="y1")
+        nc.tensor.matmul(out=shift_bank[:], lhsT=ones[:], rhs=ln_rows[:, 1, 0:D_CONTENT], start=True, stop=True)
+        tails_bank = y1_psum.tile([P, 2, D_POS], F32, tag="y1")
+        nc.tensor.matmul(out=tails_bank[:], lhsT=ones[:], rhs=ln_rows[:, :, D_CONTENT:D_MODEL], start=True, stop=True)
+        shift = const.tile([P, D_MODEL], F32)
+        gain_tail = const.tile([P, D_POS], F32)
+        nc.scalar.copy(out=shift[:, 0:D_CONTENT], in_=shift_bank[:])
+        nc.scalar.copy(out=shift[:, D_CONTENT:D_MODEL], in_=tails_bank[:, 1, :])
+        nc.scalar.copy(out=gain_tail[:], in_=tails_bank[:, 0, :])
 
-        w1_raw = const.tile([P, HEADS, D_CONTENT], BF16)
-        w2_raw = const.tile([P, HEADS, D_POS], BF16)
-        nc.sync.dma_start(out=w1_raw[0:HALF], in_=w_proj1.rearrange("(h j) n -> j h n", j=HALF))
-        nc.sync.dma_start(out=w2_raw[HALF:P], in_=w_proj2.rearrange("(h j) n -> j h n", j=HALF))
-
-        load_chunk(1)
-
-        gain = const.tile([P, D_MODEL], BF16)
-        shift = const.tile([P, D_MODEL], BF16)
-        nc.sync.dma_start(out=gain[:], in_=ln_a.partition_broadcast(P))
-        nc.sync.dma_start(out=shift[:], in_=ln_b.partition_broadcast(P))
-
-        w1_codes = const.tile([P, 4, D_CONTENT], U32, align_bytes=64)
-        w1_scales = const.tile([P, 4, D_CONTENT], U8, align_bytes=64)
-        w2_codes = const.tile([P, 4, D_POS], U32, align_bytes=64)
-        w2_scales = const.tile([P, 4, D_POS], U8, align_bytes=64)
-        w1_by_set = w1_raw[0:HALF].rearrange("p (g t r) n -> p g r n t", g=HEAD_SETS, t=PACK, r=PARITIES)
-        w2_by_set = w2_raw[HALF:P].rearrange("p (g t r) n -> p g r n t", g=HEAD_SETS, t=PACK, r=PARITIES)
-        for g in range(HEAD_SETS):
-            for r in range(PARITIES):
-                nc.vector.tensor_copy(out=w1_grouped[0:HALF, 2 * g + r], in_=w1_by_set[:, g, r])
-                nc.vector.tensor_copy(out=w2_grouped[HALF:P, 2 * g + r], in_=w2_by_set[:, g, r])
-        for q in range(4):
-            nc.vector.quantize_mx(
-                out=w1_codes[:, q, :].bitcast(FP8X4),
-                scales=w1_scales[:, q, :],
-                in_=w1_grouped[:, q].rearrange("p n t -> p (n t)"),
-            )
+        w1_codes = const.tile([P, QUADS, D_CONTENT], U32, align_bytes=64)
+        w1_scales = const.tile([P, QUADS, D_CONTENT], U8, align_bytes=64)
+        w2_codes = const.tile([P, QUADS, D_POS], U32, align_bytes=64)
+        w2_scales = const.tile([P, QUADS, D_POS], U8, align_bytes=64)
+        w1_by_quad = w1_raw[0:HALF].rearrange("p g (t r) n -> p g r n t", t=PACK, r=PARITIES)
+        w2_by_quad = w2_raw[HALF:P].rearrange("p (g t r) n -> p g r n t", g=HEAD_SETS, t=PACK, r=PARITIES)
+        for q in range(QUADS):
+            nc.scalar.copy(out=w2_grouped[HALF:P, q], in_=w2_by_quad[:, q // PARITIES, q % PARITIES])
         nc.vector.quantize_mx(
             out=w2_codes[:].rearrange("p q n -> p (q n)").bitcast(FP8X4),
             scales=w2_scales[:].rearrange("p q n -> p (q n)"),
             in_=w2_grouped[:].rearrange("p q n t -> p (q n t)"),
         )
 
+        def quantise_w1(q):
+            nc.vector.quantize_mx(
+                out=w1_codes[:, q, :].bitcast(FP8X4),
+                scales=w1_scales[:, q, :],
+                in_=w1_grouped[:, q].rearrange("p n t -> p (n t)"),
+            )
+
+        for q in range(QUADS):
+            nc.vector.tensor_copy(out=w1_grouped[0:HALF, q], in_=w1_by_quad[:, q // PARITIES, q % PARITIES])
+            if q > 0:
+                quantise_w1(q - 1)
+        quantise_w1(QUADS - 1)
+
         xg_tiles = {}
         code_tiles = {}
-        y_tiles = {}
+        y1_tiles = {}
+        y2_tiles = {}
         z_tiles = {}
-        stat_tiles = {}
+        sums_tiles = {}
+        mean_tiles = {}
         u_tiles = {}
+        sumsq_tiles = {}
+        sigma_tiles = {}
+        inv_tiles = {}
 
         def tiles_of(rnd):
             return range(rnd * ROUND, (rnd + 1) * ROUND)
@@ -138,23 +176,23 @@ def tile_multiheadattention_pa_t_kernel(tc, attn_out, inp, w_proj1, w_proj2, ln_
                     nc.scalar.copy(out=xg[:, g, :], in_=bank[:].rearrange("p c s t -> p (c s t)"))
                 xg_tiles[k] = xg
 
-        def quantise_round(rnd):
-            for k in tiles_of(rnd):
-                codes = packed.tile([P, 4, P], U32, align_bytes=64)
-                scales = packed.tile([P, 4, P], U8, align_bytes=64)
-                nc.vector.quantize_mx(
-                    out=codes[:].rearrange("p q m -> p (q m)").bitcast(FP8X4),
-                    scales=scales[:].rearrange("p q m -> p (q m)"),
-                    in_=xg_tiles[k][:].rearrange("p g w -> p (g w)"),
-                )
-                code_tiles[k] = (codes, scales)
+        def quantise(k):
+            codes = packed.tile([P, QUADS, P], U32, align_bytes=64)
+            scales = packed.tile([P, QUADS, P], U8, align_bytes=64)
+            nc.vector.quantize_mx(
+                out=codes[:].rearrange("p q m -> p (q m)").bitcast(FP8X4),
+                scales=scales[:].rearrange("p q m -> p (q m)"),
+                in_=xg_tiles[k][:].rearrange("p g w -> p (g w)"),
+            )
+            code_tiles[k] = (codes, scales)
 
         def multiply_round(rnd):
+            y2 = y2_psum.tile([P, ROUND, D_POS], F32)
+            y2_tiles[rnd] = y2
             for k in tiles_of(rnd):
                 codes, scales = code_tiles[k]
-                y1 = y_psum.tile([P, D_CONTENT], F32)
-                y2 = y_psum.tile([P, D_POS], F32)
-                for q in range(4):
+                y1 = y1_psum.tile([P, D_CONTENT], F32, tag="y1")
+                for q in range(QUADS):
                     nc.tensor.matmul_mx(
                         out=y1[:],
                         lhsT=codes[:, q, :].bitcast(FP8X4),
@@ -162,78 +200,125 @@ def tile_multiheadattention_pa_t_kernel(tc, attn_out, inp, w_proj1, w_proj2, ln_
                         rhs=w1_codes[:, q, :].bitcast(FP8X4),
                         rhs_scale=w1_scales[:, q, :],
                         start=(q == 0),
-                        stop=(q == 3),
+                        stop=(q == QUADS - 1),
                     )
-                for q in range(4):
+                for q in range(QUADS):
                     nc.tensor.matmul_mx(
-                        out=y2[:],
+                        out=y2[:, k % ROUND, :],
                         lhsT=codes[:, q, :].bitcast(FP8X4),
                         lhsT_scale=scales[:, q, :],
                         rhs=w2_codes[:, q, :].bitcast(FP8X4),
                         rhs_scale=w2_scales[:, q, :],
                         start=(q == 0),
-                        stop=(q == 3),
+                        stop=(q == QUADS - 1),
                     )
-                y_tiles[k] = (y1, y2)
+                y1_tiles[k] = y1
 
-        def residual_round(rnd):
+        def add_residual(k):
+            res = res_tiles[k // CHUNK]
+            z = zpool.tile([P, D_MODEL], F32)
+            sums = stats.tile([P, 2], F32)
+            nc.vector.scalar_tensor_tensor(
+                out=z[:, 0:D_CONTENT], in0=y1_tiles[k][:], scalar=1.0, in1=res[:, k % CHUNK, 0:D_CONTENT],
+                op0=ALU.mult, op1=ALU.add, accum_out=sums[:, 0:1],
+            )
+            nc.vector.scalar_tensor_tensor(
+                out=z[:, D_CONTENT:D_MODEL], in0=y2_tiles[k // ROUND][:, k % ROUND, :], scalar=1.0,
+                in1=res[:, k % CHUNK, D_CONTENT:D_MODEL],
+                op0=ALU.mult, op1=ALU.add, accum_out=sums[:, 1:2],
+            )
+            z_tiles[k] = z
+            sums_tiles[k] = sums
+
+        def mean(k):
+            neg_mean = stats.tile([P, 1], F32)
+            nc.vector.tensor_scalar(
+                out=neg_mean[:], in0=sums_tiles[k][:, 0:1], scalar1=sums_tiles[k][:, 1:2], scalar2=-1.0 / D_MODEL,
+                op0=ALU.add, op1=ALU.mult,
+            )
+            mean_tiles[k] = neg_mean
+
+        def centre_and_gain(k):
+            u = upool.tile([P, D_MODEL], F32)
+            nc.vector.scalar_tensor_tensor(
+                out=u[:, 0:D_CONTENT], in0=z_tiles[k][:, 0:D_CONTENT], scalar=mean_tiles[k][:, 0:1],
+                in1=gain_head[:], op0=ALU.add, op1=ALU.mult,
+            )
+            nc.vector.scalar_tensor_tensor(
+                out=u[:, D_CONTENT:D_MODEL], in0=z_tiles[k][:, D_CONTENT:D_MODEL], scalar=mean_tiles[k][:, 0:1],
+                in1=gain_tail[:], op0=ALU.add, op1=ALU.mult,
+            )
+            u_tiles[k] = u
+
+        def deviation_round(rnd):
+            sum_sq = stats.tile([P, ROUND], F32)
             for k in tiles_of(rnd):
-                y1, y2 = y_tiles[k]
-                res = res_tiles[k // CHUNK]
-                z = work.tile([P, D_MODEL], F32)
-                sums = stats.tile([P, 2], F32)
-                nc.vector.scalar_tensor_tensor(
-                    out=z[:, 0:D_CONTENT], in0=y1[:], scalar=1.0, in1=res[:, k % CHUNK, 0:D_CONTENT],
-                    op0=ALU.mult, op1=ALU.add, accum_out=sums[:, 0:1],
-                )
-                nc.vector.scalar_tensor_tensor(
-                    out=z[:, D_CONTENT:D_MODEL], in0=y2[:], scalar=1.0, in1=res[:, k % CHUNK, D_CONTENT:D_MODEL],
-                    op0=ALU.mult, op1=ALU.add, accum_out=sums[:, 1:2],
-                )
-                neg_mean = stats.tile([P, 1], F32)
-                nc.vector.tensor_scalar(
-                    out=neg_mean[:], in0=sums[:, 0:1], scalar1=sums[:, 1:2], scalar2=-1.0 / D_MODEL,
-                    op0=ALU.add, op1=ALU.mult,
-                )
-                squares = work.tile([P, D_MODEL], F32)
-                sum_sq = stats.tile([P, 1], F32)
+                squares = scratch.tile([P, D_MODEL], F32)
                 nc.scalar.activation(
-                    out=squares[:], in_=z[:], func=ACT.Square, bias=neg_mean[:, 0:1], scale=1.0,
-                    accum_out=sum_sq[:, 0:1],
+                    out=squares[:], in_=z_tiles[k][:], func=ACT.Square, bias=mean_tiles[k][:, 0:1], scale=1.0,
+                    accum_out=sum_sq[:, k % ROUND : k % ROUND + 1],
                 )
-                sigma = stats.tile([P, 1], F32)
-                nc.scalar.activation(out=sigma[:], in_=sum_sq[:], func=ACT.Sqrt, scale=1.0 / (D_MODEL - 1))
-                u = work.tile([P, D_MODEL], F32)
-                nc.vector.scalar_tensor_tensor(
-                    out=u[:], in0=z[:], scalar=neg_mean[:, 0:1], in1=gain[:], op0=ALU.add, op1=ALU.mult,
-                )
-                u_tiles[k] = u
-                stat_tiles[k] = sigma
+            sigma = stats.tile([P, ROUND], F32)
+            nc.scalar.activation(out=sigma[:], in_=sum_sq[:], func=ACT.Sqrt, scale=1.0 / (D_MODEL - 1))
+            sigma_tiles[rnd] = sigma
+
+        def add_eps(rnd):
+            sigma_eps = stats.tile([P, ROUND], F32)
+            nc.vector.tensor_scalar_add(out=sigma_eps[:], in0=sigma_tiles[rnd][:], scalar1=EPS)
+            sigma_tiles[rnd] = sigma_eps
+
+        def invert(rnd):
+            inv = stats.tile([P, ROUND], F32)
+            nc.vector.reciprocal(out=inv[:], in_=sigma_tiles[rnd][:])
+            inv_tiles[rnd] = inv
 
         def finish_round(rnd):
             o = result.tile([P, ROUND, D_MODEL], F32)
             for k in tiles_of(rnd):
-                sigma_eps = stats.tile([P, 1], F32)
-                nc.vector.tensor_scalar_add(out=sigma_eps[:], in0=stat_tiles[k][:], scalar1=EPS)
-                inv = stats.tile([P, 1], F32)
-                nc.vector.reciprocal(out=inv[:], in_=sigma_eps[:])
-                nc.vector.scalar_tensor_tensor(
-                    out=o[:, k % ROUND, :], in0=u_tiles[k][:], scalar=inv[:, 0:1], in1=shift[:],
-                    op0=ALU.mult, op1=ALU.add,
+                nc.scalar.activation(
+                    out=o[:, k % ROUND, :], in_=u_tiles[k][:], func=ACT.Copy,
+                    scale=inv_tiles[rnd][:, k % ROUND : k % ROUND + 1],
                 )
+            nc.gpsimd.tensor_tensor(
+                out=o[:], in0=o[:], in1=shift[:].unsqueeze(1).to_broadcast([P, ROUND, D_MODEL]), op=ALU.add,
+            )
             k0 = rnd * ROUND
             nc.sync.dma_start(out=out_view[:, k0 : k0 + ROUND, :], in_=o[:])
 
-        for step in range(N_ROUNDS + 3):
-            if step % 2 == 0 and step // 2 + CHUNKS_AHEAD < N_CHUNKS:
-                load_chunk(step // 2 + CHUNKS_AHEAD)
-            if step < N_ROUNDS:
+        def live(rnd):
+            return 0 <= rnd < N_ROUNDS
+
+        for step in range(N_ROUNDS + 6):
+            if step % ROUNDS_PER_CHUNK == 0:
+                c = step // ROUNDS_PER_CHUNK
+                if c + CHUNKS_AHEAD < N_CHUNKS:
+                    load_x(c + CHUNKS_AHEAD)
+                if c < N_CHUNKS:
+                    load_residual(c)
+            if live(step - 4):
+                deviation_round(step - 4)
+            if live(step - 5):
+                add_eps(step - 5)
+            if live(step - 3):
+                first, second = tiles_of(step - 3)
+                add_residual(first)
+            if live(step - 5):
+                invert(step - 5)
+            if live(step - 3):
+                add_residual(second)
+            if live(step):
                 transpose_round(step)
-            if 0 <= step - 2 < N_ROUNDS:
-                residual_round(step - 2)
-            if step < N_ROUNDS:
-                quantise_round(step)
-            if 0 <= step - 1 < N_ROUNDS:
-                multiply_round(step - 1)
-            if 0 <= step - 3 < N_ROUNDS:
-                finish_round(step - 3)
+            if live(step - 3):
+                mean(first)
+            if live(step - 1):
+                quantise((step - 1) * ROUND)
+            if live(step - 3):
+                mean(second)
+                centre_and_gain(first)
+                centre_and_gain(second)
+            if live(step - 1):
+                quantise((step - 1) * ROUND + 1)
+            if live(step - 2):
+                multiply_round(step - 2)
+            if live(step - 5):
+                finish_round(step - 5)

@@ -27,7 +27,7 @@ HEAD_SETS = 2
 PARITIES = 2
 QUADS = HEAD_SETS * PARITIES
 SLABS = 8
-ROUND = 2
+ROUND = 1
 N_ROUNDS = N_TILES // ROUND
 CHUNK = 4
 N_CHUNKS = N_TILES // CHUNK
@@ -52,8 +52,8 @@ def tile_multiheadattention_pa_t_kernel(tc, attn_out, inp, w_proj1, w_proj2, ln_
         resin = ctx.enter_context(tc.tile_pool(name="resin", bufs=3))
         grouped = ctx.enter_context(tc.tile_pool(name="grouped", bufs=6))
         packed = ctx.enter_context(tc.tile_pool(name="packed", bufs=4))
-        zpool = ctx.enter_context(tc.tile_pool(name="zpool", bufs=4))
-        upool = ctx.enter_context(tc.tile_pool(name="upool", bufs=6))
+        zpool = ctx.enter_context(tc.tile_pool(name="zpool", bufs=3 * ROUND))
+        upool = ctx.enter_context(tc.tile_pool(name="upool", bufs=3 * ROUND))
         scratch = ctx.enter_context(tc.tile_pool(name="scratch", bufs=2))
         stats = ctx.enter_context(tc.tile_pool(name="stats", bufs=8))
         result = ctx.enter_context(tc.tile_pool(name="result", bufs=3))
@@ -300,24 +300,21 @@ def tile_multiheadattention_pa_t_kernel(tc, attn_out, inp, w_proj1, w_proj2, ln_
             if live(step - 5):
                 add_eps(step - 5)
             if live(step - 3):
-                first, second = tiles_of(step - 3)
-                add_residual(first)
+                for k in tiles_of(step - 3):
+                    add_residual(k)
             if live(step - 5):
                 invert(step - 5)
-            if live(step - 3):
-                add_residual(second)
             if live(step):
                 transpose_round(step)
+            if live(step - 4):
+                for k in tiles_of(step - 4):
+                    centre_and_gain(k)
             if live(step - 3):
-                mean(first)
+                for k in tiles_of(step - 3):
+                    mean(k)
             if live(step - 1):
-                quantise((step - 1) * ROUND)
-            if live(step - 3):
-                mean(second)
-                centre_and_gain(first)
-                centre_and_gain(second)
-            if live(step - 1):
-                quantise((step - 1) * ROUND + 1)
+                for k in tiles_of(step - 1):
+                    quantise(k)
             if live(step - 2):
                 multiply_round(step - 2)
             if live(step - 5):

@@ -27,7 +27,7 @@ HEAD_SETS = 2
 PARITIES = 2
 QUADS = HEAD_SETS * PARITIES
 SLABS = 8
-ROUND = 1
+ROUND = 2
 N_ROUNDS = N_TILES // ROUND
 CHUNK = 4
 N_CHUNKS = N_TILES // CHUNK
@@ -173,7 +173,9 @@ def tile_multiheadattention_pa_t_kernel(tc, attn_out, inp, w_proj1, w_proj2, ln_
                     bank = t_psum.tile([P, P // PACK, SLABS, PACK], BF16)
                     for s in range(SLABS):
                         nc.tensor.transpose(bank[:, :, s, :], x[:, g, s, k % CHUNK, :], perm[:])
-                    nc.scalar.copy(out=xg[:, g, :], in_=bank[:].rearrange("p c s t -> p (c s t)"))
+                    nc.scalar.copy(
+                        out=xg[:, g, :].bitcast(F32), in_=bank[:].rearrange("p c s t -> p (c s t)").bitcast(F32)
+                    )
                 xg_tiles[k] = xg
 
         def quantise(k):

@@ -33,6 +33,7 @@ CHUNK = 4
 N_CHUNKS = N_TILES // CHUNK
 ROUNDS_PER_CHUNK = CHUNK // ROUND
 CHUNKS_AHEAD = 2
+SLABS_PER_LOAD = 4
 
 FLOPS = 2 * TOKENS * (HEADS * HALF) * D_MODEL
 
@@ -69,7 +70,11 @@ def tile_multiheadattention_pa_t_kernel(tc, attn_out, inp, w_proj1, w_proj2, ln_
             k0 = c * CHUNK
             x = xin.tile([P, HEAD_SETS, SLABS, CHUNK, D_V], BF16)
             for g in range(HEAD_SETS):
-                nc.sync.dma_start(out=x[:, g], in_=x_view[g, :, :, k0 : k0 + CHUNK, :])
+                for s0 in range(0, SLABS, SLABS_PER_LOAD):
+                    nc.sync.dma_start(
+                        out=x[:, g, s0 : s0 + SLABS_PER_LOAD],
+                        in_=x_view[g, :, s0 : s0 + SLABS_PER_LOAD, k0 : k0 + CHUNK, :],
+                    )
             x_tiles[c] = x
 
         def load_residual(c):
@@ -285,7 +290,7 @@ def tile_multiheadattention_pa_t_kernel(tc, attn_out, inp, w_proj1, w_proj2, ln_
                 out=o[:], in0=o[:], in1=shift[:].unsqueeze(1).to_broadcast([P, ROUND, D_MODEL]), op=ALU.add,
             )
             k0 = rnd * ROUND
-            nc.sync.dma_start(out=out_view[:, k0 : k0 + ROUND, :], in_=o[:])
+            nc.gpsimd.dma_start(out=out_view[:, k0 : k0 + ROUND, :], in_=o[:])
 
         def live(rnd):
             return 0 <= rnd < N_ROUNDS

@@ -33,7 +33,6 @@ CHUNK = 4
 N_CHUNKS = N_TILES // CHUNK
 ROUNDS_PER_CHUNK = CHUNK // ROUND
 CHUNKS_AHEAD = 2
-SLABS_PER_LOAD = 4
 
 FLOPS = 2 * TOKENS * (HEADS * HALF) * D_MODEL
 
@@ -70,11 +69,7 @@ def tile_multiheadattention_pa_t_kernel(tc, attn_out, inp, w_proj1, w_proj2, ln_
             k0 = c * CHUNK
             x = xin.tile([P, HEAD_SETS, SLABS, CHUNK, D_V], BF16)
             for g in range(HEAD_SETS):
-                for s0 in range(0, SLABS, SLABS_PER_LOAD):
-                    nc.sync.dma_start(
-                        out=x[:, g, s0 : s0 + SLABS_PER_LOAD],
-                        in_=x_view[g, :, s0 : s0 + SLABS_PER_LOAD, k0 : k0 + CHUNK, :],
-                    )
+                nc.sync.dma_start(out=x[:, g], in_=x_view[g, :, :, k0 : k0 + CHUNK, :])
             x_tiles[c] = x
 
         def load_residual(c):
@@ -175,11 +170,14 @@ def tile_multiheadattention_pa_t_kernel(tc, attn_out, inp, w_proj1, w_proj2, ln_
                 x = x_tiles[k // CHUNK]
                 xg = grouped.tile([P, HEAD_SETS, SLABS * P], BF16, align_bytes=64)
                 for g in range(HEAD_SETS):
-                    bank = t_psum.tile([P, P // PACK, SLABS, PACK], BF16)
+                    bank = t_psum.tile([P, SLABS, P], BF16)
                     for s in range(SLABS):
-                        nc.tensor.transpose(bank[:, :, s, :], x[:, g, s, k % CHUNK, :], perm[:])
+                        nc.tensor.transpose(bank[:, s, :], x[:, g, s, k % CHUNK, :], perm[:])
                     nc.scalar.copy(
-                        out=xg[:, g, :].bitcast(F32), in_=bank[:].rearrange("p c s t -> p (c s t)").bitcast(F32)
+                        out=xg[:, g, :].bitcast(F32).rearrange("p (c s w) -> p c s w", s=SLABS, w=2),
+                        in_=bank[:].rearrange("p s j -> p (s j)").bitcast(F32).rearrange(
+                            "p (s c w) -> p c s w", s=SLABS, w=2
+                        ),
                     )
                 xg_tiles[k] = xg
 
@@ -290,7 +288,7 @@ def tile_multiheadattention_pa_t_kernel(tc, attn_out, inp, w_proj1, w_proj2, ln_
                 out=o[:], in0=o[:], in1=shift[:].unsqueeze(1).to_broadcast([P, ROUND, D_MODEL]), op=ALU.add,
             )
             k0 = rnd * ROUND
-            nc.gpsimd.dma_start(out=out_view[:, k0 : k0 + ROUND, :], in_=o[:])
+            nc.sync.dma_start(out=out_view[:, k0 : k0 + ROUND, :], in_=o[:])
 
         def live(rnd):
             return 0 <= rnd < N_ROUNDS

@@ -5,6 +5,7 @@ from concourse.masks import make_identity
 
 BF16 = mybir.dt.bfloat16
 F32 = mybir.dt.float32
+I32 = mybir.dt.int32
 U32 = mybir.dt.uint32
 U8 = mybir.dt.uint8
 FP8X4 = mybir.dt.float8_e4m3fn_x4
@@ -50,17 +51,18 @@ def tile_multiheadattention_pa_t_kernel(tc, attn_out, inp, w_proj1, w_proj2, ln_
         const = ctx.enter_context(tc.tile_pool(name="const", bufs=1))
         xin = ctx.enter_context(tc.tile_pool(name="xin", bufs=3))
         resin = ctx.enter_context(tc.tile_pool(name="resin", bufs=3))
-        grouped = ctx.enter_context(tc.tile_pool(name="grouped", bufs=6))
-        packed = ctx.enter_context(tc.tile_pool(name="packed", bufs=4))
-        zpool = ctx.enter_context(tc.tile_pool(name="zpool", bufs=3 * ROUND))
+        grouped = ctx.enter_context(tc.tile_pool(name="grouped", bufs=3 * ROUND))
+        packed = ctx.enter_context(tc.tile_pool(name="packed", bufs=2 * ROUND))
+        zpool = ctx.enter_context(tc.tile_pool(name="zpool", bufs=2 * ROUND))
+        cpool = ctx.enter_context(tc.tile_pool(name="cpool", bufs=3 * ROUND))
         upool = ctx.enter_context(tc.tile_pool(name="upool", bufs=3 * ROUND))
         scratch = ctx.enter_context(tc.tile_pool(name="scratch", bufs=2))
         stats = ctx.enter_context(tc.tile_pool(name="stats", bufs=8))
         result = ctx.enter_context(tc.tile_pool(name="result", bufs=3))
-        t_psum = ctx.enter_context(tc.psum_pool(name="t_psum", bufs=4))
-        y1_psum = ctx.enter_context(tc.psum_pool(name="y1_psum", bufs=2))
+        t_psum = ctx.enter_context(tc.psum_pool(name="t_psum", bufs=HEAD_SETS * ROUND))
+        y1_psum = ctx.enter_context(tc.psum_pool(name="y1_psum", bufs=ROUND))
         y2_psum = ctx.enter_context(tc.psum_pool(name="y2_psum", bufs=1))
-        gain_psum = ctx.enter_context(tc.psum_pool(name="gain_psum", bufs=1))
+        shift_psum = ctx.enter_context(tc.psum_pool(name="shift_psum", bufs=1))
 
         x_tiles = {}
         res_tiles = {}
@@ -93,16 +95,6 @@ def tile_multiheadattention_pa_t_kernel(tc, attn_out, inp, w_proj1, w_proj2, ln_
 
         ones = const.tile([P, P], BF16)
         nc.vector.memset(ones[:], 1.0)
-        w1_grouped = const.tile([P, QUADS, D_CONTENT, PACK], BF16, align_bytes=64)
-        w2_grouped = const.tile([P, QUADS, D_POS, PACK], BF16, align_bytes=64)
-        nc.vector.memset(w1_grouped[HALF:P], 0.0)
-        nc.vector.memset(w2_grouped[0:HALF], 0.0)
-
-        warm = const.tile([P, 1], F32)
-        nc.vector.memset(warm[:], 1.0)
-        warm_out = const.tile([P, 1], F32)
-        nc.scalar.activation(out=warm_out[:], in_=warm[:], func=ACT.Sqrt)
-
         ident = const.tile([P, P], BF16)
         make_identity(nc, ident[:])
         perm = const.tile([P, P], BF16)
@@ -110,18 +102,27 @@ def tile_multiheadattention_pa_t_kernel(tc, attn_out, inp, w_proj1, w_proj2, ln_
             out=perm[:].rearrange("p (c t) -> p c t", t=PACK),
             in_=ident[:].rearrange("p (t c) -> p c t", t=PACK),
         )
+        warm = const.tile([P, 1], F32)
+        nc.vector.memset(warm[:], 1.0)
+        warm_out = const.tile([P, 1], F32)
+        nc.scalar.activation(out=warm_out[:], in_=warm[:], func=ACT.Sqrt)
 
-        gain_head = gain_psum.tile([P, D_CONTENT], F32)
-        nc.tensor.matmul(out=gain_head[:], lhsT=ones[:], rhs=ln_rows[:, 0, 0:D_CONTENT], start=True, stop=True)
-        shift_bank = y1_psum.tile([P, D_CONTENT], F32, tag="y1")
-        nc.tensor.matmul(out=shift_bank[:], lhsT=ones[:], rhs=ln_rows[:, 1, 0:D_CONTENT], start=True, stop=True)
+        w1_grouped = const.tile([P, QUADS, D_CONTENT, PACK], BF16, align_bytes=64)
+        w2_grouped = const.tile([P, QUADS, D_POS, PACK], BF16, align_bytes=64)
+        nc.vector.memset(w2_grouped[0:HALF].rearrange("p q n t -> p (q n t)").bitcast(I32), 0)
+        nc.vector.memset(w1_grouped[HALF:P].rearrange("p q n t -> p (q n t)").bitcast(I32), 0)
+
+        shift_head = shift_psum.tile([P, D_CONTENT], F32)
+        nc.tensor.matmul(out=shift_head[:], lhsT=ones[:], rhs=ln_rows[:, 1, 0:D_CONTENT], start=True, stop=True)
+        gain_bank = y1_psum.tile([P, D_CONTENT], F32, tag="y1")
+        nc.tensor.matmul(out=gain_bank[:], lhsT=ones[:], rhs=ln_rows[:, 0, 0:D_CONTENT], start=True, stop=True)
         tails_bank = y1_psum.tile([P, 2, D_POS], F32, tag="y1")
         nc.tensor.matmul(out=tails_bank[:], lhsT=ones[:], rhs=ln_rows[:, :, D_CONTENT:D_MODEL], start=True, stop=True)
-        shift = const.tile([P, D_MODEL], F32)
-        gain_tail = const.tile([P, D_POS], F32)
-        nc.scalar.copy(out=shift[:, 0:D_CONTENT], in_=shift_bank[:])
-        nc.scalar.copy(out=shift[:, D_CONTENT:D_MODEL], in_=tails_bank[:, 1, :])
-        nc.scalar.copy(out=gain_tail[:], in_=tails_bank[:, 0, :])
+        gain = const.tile([P, D_MODEL], F32)
+        shift_tail = const.tile([P, D_POS], F32)
+        nc.scalar.copy(out=gain[:, 0:D_CONTENT], in_=gain_bank[:])
+        nc.scalar.copy(out=gain[:, D_CONTENT:D_MODEL], in_=tails_bank[:, 0, :])
+        nc.scalar.copy(out=shift_tail[:], in_=tails_bank[:, 1, :])
 
         w1_codes = const.tile([P, QUADS, D_CONTENT], U32, align_bytes=64)
         w1_scales = const.tile([P, QUADS, D_CONTENT], U8, align_bytes=64)
@@ -157,8 +158,8 @@ def tile_multiheadattention_pa_t_kernel(tc, attn_out, inp, w_proj1, w_proj2, ln_
         z_tiles = {}
         sums_tiles = {}
         mean_tiles = {}
+        zc_tiles = {}
         u_tiles = {}
-        sumsq_tiles = {}
         sigma_tiles = {}
         inv_tiles = {}
 
@@ -167,19 +168,18 @@ def tile_multiheadattention_pa_t_kernel(tc, attn_out, inp, w_proj1, w_proj2, ln_
 
         def transpose_round(rnd):
             for k in tiles_of(rnd):
-                x = x_tiles[k // CHUNK]
                 xg = grouped.tile([P, HEAD_SETS, SLABS * P], BF16, align_bytes=64)
-                for g in range(HEAD_SETS):
-                    bank = t_psum.tile([P, SLABS, P], BF16)
-                    for s in range(SLABS):
-                        nc.tensor.transpose(bank[:, s, :], x[:, g, s, k % CHUNK, :], perm[:])
-                    nc.scalar.copy(
-                        out=xg[:, g, :].bitcast(F32).rearrange("p (c s w) -> p c s w", s=SLABS, w=2),
-                        in_=bank[:].rearrange("p s j -> p (s j)").bitcast(F32).rearrange(
-                            "p (s c w) -> p c s w", s=SLABS, w=2
-                        ),
-                    )
                 xg_tiles[k] = xg
+            for g in range(HEAD_SETS):
+                for k in tiles_of(rnd):
+                    x = x_tiles[k // CHUNK]
+                    bank = t_psum.tile([P, P // PACK, SLABS, PACK], BF16)
+                    for s in range(SLABS):
+                        nc.tensor.transpose(bank[:, :, s, :], x[:, g, s, k % CHUNK, :], perm[:])
+                    nc.scalar.copy(
+                        out=xg_tiles[k][:, g, :].bitcast(F32),
+                        in_=bank[:].rearrange("p c s t -> p (c s t)").bitcast(F32),
+                    )
 
         def quantise(k):
             codes = packed.tile([P, QUADS, P], U32, align_bytes=64)
@@ -243,16 +243,19 @@ def tile_multiheadattention_pa_t_kernel(tc, attn_out, inp, w_proj1, w_proj2, ln_
             )
             mean_tiles[k] = neg_mean
 
-        def centre_and_gain(k):
+        def centre(k):
+            zc = cpool.tile([P, D_MODEL], F32)
+            if k % 2 == 0:
+                nc.scalar.activation(out=zc[:], in_=z_tiles[k][:], func=ACT.Identity, bias=mean_tiles[k][:, 0:1], scale=1.0)
+            else:
+                nc.gpsimd.tensor_scalar(
+                    out=zc[:], in0=z_tiles[k][:], scalar1=mean_tiles[k][:, 0:1], scalar2=1.0, op0=ALU.add, op1=ALU.mult,
+                )
+            zc_tiles[k] = zc
+
+        def apply_gain(k):
             u = upool.tile([P, D_MODEL], F32)
-            nc.vector.scalar_tensor_tensor(
-                out=u[:, 0:D_CONTENT], in0=z_tiles[k][:, 0:D_CONTENT], scalar=mean_tiles[k][:, 0:1],
-                in1=gain_head[:], op0=ALU.add, op1=ALU.mult,
-            )
-            nc.vector.scalar_tensor_tensor(
-                out=u[:, D_CONTENT:D_MODEL], in0=z_tiles[k][:, D_CONTENT:D_MODEL], scalar=mean_tiles[k][:, 0:1],
-                in1=gain_tail[:], op0=ALU.add, op1=ALU.mult,
-            )
+            nc.gpsimd.tensor_tensor(out=u[:], in0=zc_tiles[k][:], in1=gain[:], op=ALU.mult)
             u_tiles[k] = u
 
         def deviation_round(rnd):
@@ -260,40 +263,39 @@ def tile_multiheadattention_pa_t_kernel(tc, attn_out, inp, w_proj1, w_proj2, ln_
             for k in tiles_of(rnd):
                 squares = scratch.tile([P, D_MODEL], F32)
                 nc.scalar.activation(
-                    out=squares[:], in_=z_tiles[k][:], func=ACT.Square, bias=mean_tiles[k][:, 0:1], scale=1.0,
+                    out=squares[:], in_=zc_tiles[k][:], func=ACT.Square,
                     accum_out=sum_sq[:, k % ROUND : k % ROUND + 1],
                 )
             sigma = stats.tile([P, ROUND], F32)
             nc.scalar.activation(out=sigma[:], in_=sum_sq[:], func=ACT.Sqrt, scale=1.0 / (D_MODEL - 1))
             sigma_tiles[rnd] = sigma
 
-        def add_eps(rnd):
+        def invert_round(rnd):
             sigma_eps = stats.tile([P, ROUND], F32)
             nc.vector.tensor_scalar_add(out=sigma_eps[:], in0=sigma_tiles[rnd][:], scalar1=EPS)
-            sigma_tiles[rnd] = sigma_eps
-
-        def invert(rnd):
             inv = stats.tile([P, ROUND], F32)
-            nc.vector.reciprocal(out=inv[:], in_=sigma_tiles[rnd][:])
+            nc.vector.reciprocal(out=inv[:], in_=sigma_eps[:])
             inv_tiles[rnd] = inv
 
         def finish_round(rnd):
             o = result.tile([P, ROUND, D_MODEL], F32)
             for k in tiles_of(rnd):
-                nc.scalar.activation(
-                    out=o[:, k % ROUND, :], in_=u_tiles[k][:], func=ACT.Copy,
-                    scale=inv_tiles[rnd][:, k % ROUND : k % ROUND + 1],
+                j = k % ROUND
+                nc.vector.scalar_tensor_tensor(
+                    out=o[:, j, 0:D_CONTENT], in0=u_tiles[k][:, 0:D_CONTENT], scalar=inv_tiles[rnd][:, j : j + 1],
+                    in1=shift_head[:], op0=ALU.mult, op1=ALU.add,
                 )
-            nc.gpsimd.tensor_tensor(
-                out=o[:], in0=o[:], in1=shift[:].unsqueeze(1).to_broadcast([P, ROUND, D_MODEL]), op=ALU.add,
-            )
+                nc.vector.scalar_tensor_tensor(
+                    out=o[:, j, D_CONTENT:D_MODEL], in0=u_tiles[k][:, D_CONTENT:D_MODEL],
+                    scalar=inv_tiles[rnd][:, j : j + 1], in1=shift_tail[:], op0=ALU.mult, op1=ALU.add,
+                )
             k0 = rnd * ROUND
             nc.sync.dma_start(out=out_view[:, k0 : k0 + ROUND, :], in_=o[:])
 
         def live(rnd):
             return 0 <= rnd < N_ROUNDS
 
-        for step in range(N_ROUNDS + 6):
+        for step in range(N_ROUNDS + 5):
             if step % ROUNDS_PER_CHUNK == 0:
                 c = step // ROUNDS_PER_CHUNK
                 if c + CHUNKS_AHEAD < N_CHUNKS:
@@ -302,25 +304,23 @@ def tile_multiheadattention_pa_t_kernel(tc, attn_out, inp, w_proj1, w_proj2, ln_
                     load_residual(c)
             if live(step - 4):
                 deviation_round(step - 4)
-            if live(step - 5):
-                add_eps(step - 5)
             if live(step - 3):
                 for k in tiles_of(step - 3):
                     add_residual(k)
-            if live(step - 5):
-                invert(step - 5)
-            if live(step):
-                transpose_round(step)
-            if live(step - 4):
-                for k in tiles_of(step - 4):
-                    centre_and_gain(k)
-            if live(step - 3):
                 for k in tiles_of(step - 3):
                     mean(k)
+            if live(step):
+                transpose_round(step)
+            if live(step - 3):
+                for k in reversed(tiles_of(step - 3)):
+                    centre(k)
+                for k in reversed(tiles_of(step - 3)):
+                    apply_gain(k)
+            if live(step - 4):
+                invert_round(step - 4)
+                finish_round(step - 4)
             if live(step - 1):
                 for k in tiles_of(step - 1):
                     quantise(k)
             if live(step - 2):
                 multiply_round(step - 2)
-            if live(step - 5):
-                finish_round(step - 5)

@@ -54,15 +54,13 @@ def tile_multiheadattention_pa_t_kernel(tc, attn_out, inp, w_proj1, w_proj2, ln_
         grouped = ctx.enter_context(tc.tile_pool(name="grouped", bufs=3 * ROUND))
         packed = ctx.enter_context(tc.tile_pool(name="packed", bufs=2 * ROUND))
         zpool = ctx.enter_context(tc.tile_pool(name="zpool", bufs=2 * ROUND))
-        cpool = ctx.enter_context(tc.tile_pool(name="cpool", bufs=3 * ROUND))
         upool = ctx.enter_context(tc.tile_pool(name="upool", bufs=3 * ROUND))
         scratch = ctx.enter_context(tc.tile_pool(name="scratch", bufs=2))
         stats = ctx.enter_context(tc.tile_pool(name="stats", bufs=8))
         result = ctx.enter_context(tc.tile_pool(name="result", bufs=3))
         t_psum = ctx.enter_context(tc.psum_pool(name="t_psum", bufs=HEAD_SETS * ROUND))
         y1_psum = ctx.enter_context(tc.psum_pool(name="y1_psum", bufs=ROUND))
-        y2_psum = ctx.enter_context(tc.psum_pool(name="y2_psum", bufs=1))
-        shift_psum = ctx.enter_context(tc.psum_pool(name="shift_psum", bufs=1))
+        y2_psum = ctx.enter_context(tc.psum_pool(name="y2_psum", bufs=2))
 
         x_tiles = {}
         res_tiles = {}
@@ -112,17 +110,18 @@ def tile_multiheadattention_pa_t_kernel(tc, attn_out, inp, w_proj1, w_proj2, ln_
         nc.vector.memset(w2_grouped[0:HALF].rearrange("p q n t -> p (q n t)").bitcast(I32), 0)
         nc.vector.memset(w1_grouped[HALF:P].rearrange("p q n t -> p (q n t)").bitcast(I32), 0)
 
-        shift_head = shift_psum.tile([P, D_CONTENT], F32)
-        nc.tensor.matmul(out=shift_head[:], lhsT=ones[:], rhs=ln_rows[:, 1, 0:D_CONTENT], start=True, stop=True)
         gain_bank = y1_psum.tile([P, D_CONTENT], F32, tag="y1")
         nc.tensor.matmul(out=gain_bank[:], lhsT=ones[:], rhs=ln_rows[:, 0, 0:D_CONTENT], start=True, stop=True)
-        tails_bank = y1_psum.tile([P, 2, D_POS], F32, tag="y1")
+        shift_bank = y1_psum.tile([P, D_CONTENT], F32, tag="y1")
+        nc.tensor.matmul(out=shift_bank[:], lhsT=ones[:], rhs=ln_rows[:, 1, 0:D_CONTENT], start=True, stop=True)
+        tails_bank = y2_psum.tile([P, 2, D_POS], F32, tag="y2")
         nc.tensor.matmul(out=tails_bank[:], lhsT=ones[:], rhs=ln_rows[:, :, D_CONTENT:D_MODEL], start=True, stop=True)
         gain = const.tile([P, D_MODEL], F32)
-        shift_tail = const.tile([P, D_POS], F32)
+        shift = const.tile([P, D_MODEL], F32)
         nc.scalar.copy(out=gain[:, 0:D_CONTENT], in_=gain_bank[:])
+        nc.scalar.copy(out=shift[:, 0:D_CONTENT], in_=shift_bank[:])
         nc.scalar.copy(out=gain[:, D_CONTENT:D_MODEL], in_=tails_bank[:, 0, :])
-        nc.scalar.copy(out=shift_tail[:], in_=tails_bank[:, 1, :])
+        nc.scalar.copy(out=shift[:, D_CONTENT:D_MODEL], in_=tails_bank[:, 1, :])
 
         w1_codes = const.tile([P, QUADS, D_CONTENT], U32, align_bytes=64)
         w1_scales = const.tile([P, QUADS, D_CONTENT], U8, align_bytes=64)
@@ -158,7 +157,6 @@ def tile_multiheadattention_pa_t_kernel(tc, attn_out, inp, w_proj1, w_proj2, ln_
         z_tiles = {}
         sums_tiles = {}
         mean_tiles = {}
-        zc_tiles = {}
         u_tiles = {}
         sigma_tiles = {}
         inv_tiles = {}
@@ -192,7 +190,7 @@ def tile_multiheadattention_pa_t_kernel(tc, attn_out, inp, w_proj1, w_proj2, ln_
             code_tiles[k] = (codes, scales)
 
         def multiply_round(rnd):
-            y2 = y2_psum.tile([P, ROUND, D_POS], F32)
+            y2 = y2_psum.tile([P, ROUND, D_POS], F32, tag="y2")
             y2_tiles[rnd] = y2
             for k in tiles_of(rnd):
                 codes, scales = code_tiles[k]
@@ -236,26 +234,18 @@ def tile_multiheadattention_pa_t_kernel(tc, attn_out, inp, w_proj1, w_proj2, ln_
             sums_tiles[k] = sums
 
         def mean(k):
+            scaled_sums = stats.tile([P, 2], F32)
             neg_mean = stats.tile([P, 1], F32)
-            nc.vector.tensor_scalar(
-                out=neg_mean[:], in0=sums_tiles[k][:, 0:1], scalar1=sums_tiles[k][:, 1:2], scalar2=-1.0 / D_MODEL,
-                op0=ALU.add, op1=ALU.mult,
+            nc.scalar.activation(
+                out=scaled_sums[:], in_=sums_tiles[k][:], func=ACT.Copy, scale=-1.0 / D_MODEL, accum_out=neg_mean[:, 0:1],
             )
             mean_tiles[k] = neg_mean
 
-        def centre(k):
-            zc = cpool.tile([P, D_MODEL], F32)
-            if k % 2 == 0:
-                nc.scalar.activation(out=zc[:], in_=z_tiles[k][:], func=ACT.Identity, bias=mean_tiles[k][:, 0:1], scale=1.0)
-            else:
-                nc.gpsimd.tensor_scalar(
-                    out=zc[:], in0=z_tiles[k][:], scalar1=mean_tiles[k][:, 0:1], scalar2=1.0, op0=ALU.add, op1=ALU.mult,
-                )
-            zc_tiles[k] = zc
-
-        def apply_gain(k):
+        def centre_and_gain(k):
             u = upool.tile([P, D_MODEL], F32)
-            nc.gpsimd.tensor_tensor(out=u[:], in0=zc_tiles[k][:], in1=gain[:], op=ALU.mult)
+            nc.vector.scalar_tensor_tensor(
+                out=u[:], in0=z_tiles[k][:], scalar=mean_tiles[k][:, 0:1], in1=gain[:], op0=ALU.add, op1=ALU.mult,
+            )
             u_tiles[k] = u
 
         def deviation_round(rnd):
@@ -263,18 +253,18 @@ def tile_multiheadattention_pa_t_kernel(tc, attn_out, inp, w_proj1, w_proj2, ln_
             for k in tiles_of(rnd):
                 squares = scratch.tile([P, D_MODEL], F32)
                 nc.scalar.activation(
-                    out=squares[:], in_=zc_tiles[k][:], func=ACT.Square,
+                    out=squares[:], in_=z_tiles[k][:], func=ACT.Square, bias=mean_tiles[k][:, 0:1], scale=1.0,
                     accum_out=sum_sq[:, k % ROUND : k % ROUND + 1],
                 )
             sigma = stats.tile([P, ROUND], F32)
             nc.scalar.activation(out=sigma[:], in_=sum_sq[:], func=ACT.Sqrt, scale=1.0 / (D_MODEL - 1))
-            sigma_tiles[rnd] = sigma
+            sigma_eps = stats.tile([P, ROUND], F32)
+            nc.scalar.activation(out=sigma_eps[:], in_=sigma[:], func=ACT.Identity, bias=EPS, scale=1.0)
+            sigma_tiles[rnd] = sigma_eps
 
         def invert_round(rnd):
-            sigma_eps = stats.tile([P, ROUND], F32)
-            nc.vector.tensor_scalar_add(out=sigma_eps[:], in0=sigma_tiles[rnd][:], scalar1=EPS)
             inv = stats.tile([P, ROUND], F32)
-            nc.vector.reciprocal(out=inv[:], in_=sigma_eps[:])
+            nc.vector.reciprocal(out=inv[:], in_=sigma_tiles[rnd][:])
             inv_tiles[rnd] = inv
 
         def finish_round(rnd):
@@ -282,12 +272,8 @@ def tile_multiheadattention_pa_t_kernel(tc, attn_out, inp, w_proj1, w_proj2, ln_
             for k in tiles_of(rnd):
                 j = k % ROUND
                 nc.vector.scalar_tensor_tensor(
-                    out=o[:, j, 0:D_CONTENT], in0=u_tiles[k][:, 0:D_CONTENT], scalar=inv_tiles[rnd][:, j : j + 1],
-                    in1=shift_head[:], op0=ALU.mult, op1=ALU.add,
-                )
-                nc.vector.scalar_tensor_tensor(
-                    out=o[:, j, D_CONTENT:D_MODEL], in0=u_tiles[k][:, D_CONTENT:D_MODEL],
-                    scalar=inv_tiles[rnd][:, j : j + 1], in1=shift_tail[:], op0=ALU.mult, op1=ALU.add,
+                    out=o[:, j, :], in0=u_tiles[k][:], scalar=inv_tiles[rnd][:, j : j + 1], in1=shift[:],
+                    op0=ALU.mult, op1=ALU.add,
                 )
             k0 = rnd * ROUND
             nc.sync.dma_start(out=out_view[:, k0 : k0 + ROUND, :], in_=o[:])
@@ -303,22 +289,21 @@ def tile_multiheadattention_pa_t_kernel(tc, attn_out, inp, w_proj1, w_proj2, ln_
                 if c < N_CHUNKS:
                     load_residual(c)
             if live(step - 4):
-                deviation_round(step - 4)
+                invert_round(step - 4)
             if live(step - 3):
                 for k in tiles_of(step - 3):
                     add_residual(k)
-                for k in tiles_of(step - 3):
-                    mean(k)
             if live(step):
                 transpose_round(step)
             if live(step - 3):
-                for k in reversed(tiles_of(step - 3)):
-                    centre(k)
-                for k in reversed(tiles_of(step - 3)):
-                    apply_gain(k)
+                for k in tiles_of(step - 3):
+                    mean(k)
+                deviation_round(step - 3)
             if live(step - 4):
-                invert_round(step - 4)
                 finish_round(step - 4)
+            if live(step - 3):
+                for k in tiles_of(step - 3):
+                    centre_and_gain(k)
             if live(step - 1):
                 for k in tiles_of(step - 1):
                     quantise(k)

from contextlib import ExitStack

import concourse.mybir as mybir
from concourse.masks import make_identity

BF16 = mybir.dt.bfloat16
F32 = mybir.dt.float32
I32 = mybir.dt.int32
U32 = mybir.dt.uint32
U8 = mybir.dt.uint8
FP8X4 = mybir.dt.float8_e4m3fn_x4
ALU = mybir.AluOpType
ACT = mybir.ActivationFunctionType

P = 128
PACK = 4
HEADS = 16
TOKENS = 4096
D_V = 128
HALF = 64
D_CONTENT = 512
D_POS = 128
D_MODEL = D_CONTENT + D_POS
EPS = 1e-3

N_TILES = TOKENS // P
HEAD_SETS = 2
PARITIES = 2
QUADS = HEAD_SETS * PARITIES
SLABS = 8
ROUND = 2
N_ROUNDS = N_TILES // ROUND
CHUNK = 4
N_CHUNKS = N_TILES // CHUNK
ROUNDS_PER_CHUNK = CHUNK // ROUND
CHUNKS_AHEAD = 2

FLOPS = 2 * TOKENS * (HEADS * HALF) * D_MODEL


def tile_multiheadattention_pa_t_kernel(tc, attn_out, inp, w_proj1, w_proj2, ln_a, ln_b, out):
    nc = tc.nc
    x_view = attn_out.flatten_outer_dims().rearrange(
        "(g p s k) f -> g p s k f", g=HEAD_SETS, p=P, s=SLABS
    )
    inp_view = inp.rearrange("(m k) c -> m k c", k=N_TILES)
    out_view = out.rearrange("(m k) c -> m k c", k=N_TILES)

    with ExitStack() as ctx:
        ctx.enter_context(tc.manual_schedule())
        const = ctx.enter_context(tc.tile_pool(name="const", bufs=1))
        xin = ctx.enter_context(tc.tile_pool(name="xin", bufs=3))
        resin = ctx.enter_context(tc.tile_pool(name="resin", bufs=3))
        grouped = ctx.enter_context(tc.tile_pool(name="grouped", bufs=3 * ROUND))
        packed = ctx.enter_context(tc.tile_pool(name="packed", bufs=2 * ROUND))
        zpool = ctx.enter_context(tc.tile_pool(name="zpool", bufs=2 * ROUND))
        upool = ctx.enter_context(tc.tile_pool(name="upool", bufs=3 * ROUND))
        scratch = ctx.enter_context(tc.tile_pool(name="scratch", bufs=2))
        stats = ctx.enter_context(tc.tile_pool(name="stats", bufs=8))
        result = ctx.enter_context(tc.tile_pool(name="result", bufs=3))
        t_psum = ctx.enter_context(tc.psum_pool(name="t_psum", bufs=HEAD_SETS * ROUND))
        y1_psum = ctx.enter_context(tc.psum_pool(name="y1_psum", bufs=ROUND))
        y2_psum = ctx.enter_context(tc.psum_pool(name="y2_psum", bufs=2))

        x_tiles = {}
        res_tiles = {}

        def load_x(c):
            k0 = c * CHUNK
            x = xin.tile([P, HEAD_SETS, SLABS, CHUNK, D_V], BF16)
            for g in range(HEAD_SETS):
                nc.sync.dma_start(out=x[:, g], in_=x_view[g, :, :, k0 : k0 + CHUNK, :])
            x_tiles[c] = x

        def load_residual(c):
            k0 = c * CHUNK
            res = resin.tile([P, CHUNK, D_MODEL], BF16)
            nc.sync.dma_start(out=res[:], in_=inp_view[:, k0 : k0 + CHUNK, :])
            res_tiles[c] = res

        ln_rows = const.tile([P, 2, D_MODEL], BF16)
        nc.vector.memset(ln_rows[:], 0.0)
        nc.sync.dma_start(out=ln_rows[0:1, 0, :], in_=ln_a.unsqueeze(0))
        nc.sync.dma_start(out=ln_rows[0:1, 1, :], in_=ln_b.unsqueeze(0))
        w1_raw = const.tile([P, HEAD_SETS, HEADS // HEAD_SETS, D_CONTENT], BF16)
        w2_raw = const.tile([P, HEADS, D_POS], BF16)
        nc.sync.dma_start(out=w2_raw[HALF:P], in_=w_proj2.rearrange("(h j) n -> j h n", j=HALF))
        load_x(0)
        w1_view = w_proj1.rearrange("(g h j) n -> g j h n", g=HEAD_SETS, j=HALF)
        for g in range(HEAD_SETS):
            nc.sync.dma_start(out=w1_raw[0:HALF, g], in_=w1_view[g])
        load_x(1)

        ones = const.tile([P, P], BF16)
        nc.vector.memset(ones[:], 1.0)
        ident = const.tile([P, P], BF16)
        make_identity(nc, ident[:])
        perm = const.tile([P, P], BF16)
        nc.vector.tensor_copy(
            out=perm[:].rearrange("p (c t) -> p c t", t=PACK),
            in_=ident[:].rearrange("p (t c) -> p c t", t=PACK),
        )
        warm = const.tile([P, 1], F32)
        nc.vector.memset(warm[:], 1.0)
        warm_out = const.tile([P, 1], F32)
        nc.scalar.activation(out=warm_out[:], in_=warm[:], func=ACT.Sqrt)

        w1_grouped = const.tile([P, QUADS, D_CONTENT, PACK], BF16, align_bytes=64)
        w2_grouped = const.tile([P, QUADS, D_POS, PACK], BF16, align_bytes=64)
        nc.vector.memset(w2_grouped[0:HALF].rearrange("p q n t -> p (q n t)").bitcast(I32), 0)
        nc.vector.memset(w1_grouped[HALF:P].rearrange("p q n t -> p (q n t)").bitcast(I32), 0)

        gain_bank = y1_psum.tile([P, D_CONTENT], F32, tag="y1")
        nc.tensor.matmul(out=gain_bank[:], lhsT=ones[:], rhs=ln_rows[:, 0, 0:D_CONTENT], start=True, stop=True)
        shift_bank = y1_psum.tile([P, D_CONTENT], F32, tag="y1")
        nc.tensor.matmul(out=shift_bank[:], lhsT=ones[:], rhs=ln_rows[:, 1, 0:D_CONTENT], start=True, stop=True)
        tails_bank = y2_psum.tile([P, 2, D_POS], F32, tag="y2")
        nc.tensor.matmul(out=tails_bank[:], lhsT=ones[:], rhs=ln_rows[:, :, D_CONTENT:D_MODEL], start=True, stop=True)
        gain = const.tile([P, D_MODEL], F32)
        shift = const.tile([P, D_MODEL], F32)
        nc.scalar.copy(out=gain[:, 0:D_CONTENT], in_=gain_bank[:])
        nc.scalar.copy(out=shift[:, 0:D_CONTENT], in_=shift_bank[:])
        nc.scalar.copy(out=gain[:, D_CONTENT:D_MODEL], in_=tails_bank[:, 0, :])
        nc.scalar.copy(out=shift[:, D_CONTENT:D_MODEL], in_=tails_bank[:, 1, :])

        w1_codes = const.tile([P, QUADS, D_CONTENT], U32, align_bytes=64)
        w1_scales = const.tile([P, QUADS, D_CONTENT], U8, align_bytes=64)
        w2_codes = const.tile([P, QUADS, D_POS], U32, align_bytes=64)
        w2_scales = const.tile([P, QUADS, D_POS], U8, align_bytes=64)
        w1_by_quad = w1_raw[0:HALF].rearrange("p g (t r) n -> p g r n t", t=PACK, r=PARITIES)
        w2_by_quad = w2_raw[HALF:P].rearrange("p (g t r) n -> p g r n t", g=HEAD_SETS, t=PACK, r=PARITIES)
        for q in range(QUADS):
            nc.scalar.copy(out=w2_grouped[HALF:P, q], in_=w2_by_quad[:, q // PARITIES, q % PARITIES])
        nc.vector.quantize_mx(
            out=w2_codes[:].rearrange("p q n -> p (q n)").bitcast(FP8X4),
            scales=w2_scales[:].rearrange("p q n -> p (q n)"),
            in_=w2_grouped[:].rearrange("p q n t -> p (q n t)"),
        )

        def quantise_w1(q):
            nc.vector.quantize_mx(
                out=w1_codes[:, q, :].bitcast(FP8X4),
                scales=w1_scales[:, q, :],
                in_=w1_grouped[:, q].rearrange("p n t -> p (n t)"),
            )

        for q in range(QUADS):
            nc.vector.tensor_copy(out=w1_grouped[0:HALF, q], in_=w1_by_quad[:, q // PARITIES, q % PARITIES])
            if q > 0:
                quantise_w1(q - 1)
        quantise_w1(QUADS - 1)

        xg_tiles = {}
        code_tiles = {}
        y1_tiles = {}
        y2_tiles = {}
        z_tiles = {}
        sums_tiles = {}
        mean_tiles = {}
        u_tiles = {}
        sigma_tiles = {}
        inv_tiles = {}

        def tiles_of(rnd):
            return range(rnd * ROUND, (rnd + 1) * ROUND)

        def transpose_round(rnd):
            for k in tiles_of(rnd):
                xg = grouped.tile([P, HEAD_SETS, SLABS * P], BF16, align_bytes=64)
                xg_tiles[k] = xg
            for g in range(HEAD_SETS):
                for k in tiles_of(rnd):
                    x = x_tiles[k // CHUNK]
                    bank = t_psum.tile([P, P // PACK, SLABS, PACK], BF16)
                    for s in range(SLABS):
                        nc.tensor.transpose(bank[:, :, s, :], x[:, g, s, k % CHUNK, :], perm[:])
                    nc.scalar.copy(
                        out=xg_tiles[k][:, g, :].bitcast(F32),
                        in_=bank[:].rearrange("p c s t -> p (c s t)").bitcast(F32),
                    )

        def quantise(k):
            codes = packed.tile([P, QUADS, P], U32, align_bytes=64)
            scales = packed.tile([P, QUADS, P], U8, align_bytes=64)
            nc.vector.quantize_mx(
                out=codes[:].rearrange("p q m -> p (q m)").bitcast(FP8X4),
                scales=scales[:].rearrange("p q m -> p (q m)"),
                in_=xg_tiles[k][:].rearrange("p g w -> p (g w)"),
            )
            code_tiles[k] = (codes, scales)

        def multiply_round(rnd):
            y2 = y2_psum.tile([P, ROUND, D_POS], F32, tag="y2")
            y2_tiles[rnd] = y2
            for k in tiles_of(rnd):
                codes, scales = code_tiles[k]
                y1 = y1_psum.tile([P, D_CONTENT], F32, tag="y1")
                for q in range(QUADS):
                    nc.tensor.matmul_mx(
                        out=y1[:],
                        lhsT=codes[:, q, :].bitcast(FP8X4),
                        lhsT_scale=scales[:, q, :],
                        rhs=w1_codes[:, q, :].bitcast(FP8X4),
                        rhs_scale=w1_scales[:, q, :],
                        start=(q == 0),
                        stop=(q == QUADS - 1),
                    )
                for q in range(QUADS):
                    nc.tensor.matmul_mx(
                        out=y2[:, k % ROUND, :],
                        lhsT=codes[:, q, :].bitcast(FP8X4),
                        lhsT_scale=scales[:, q, :],
                        rhs=w2_codes[:, q, :].bitcast(FP8X4),
                        rhs_scale=w2_scales[:, q, :],
                        start=(q == 0),
                        stop=(q == QUADS - 1),
                    )
                y1_tiles[k] = y1

        def add_residual(k):
            res = res_tiles[k // CHUNK]
            z = zpool.tile([P, D_MODEL], F32)
            sums = stats.tile([P, 2], F32)
            nc.vector.scalar_tensor_tensor(
                out=z[:, 0:D_CONTENT], in0=y1_tiles[k][:], scalar=1.0, in1=res[:, k % CHUNK, 0:D_CONTENT],
                op0=ALU.mult, op1=ALU.add, accum_out=sums[:, 0:1],
            )
            nc.vector.scalar_tensor_tensor(
                out=z[:, D_CONTENT:D_MODEL], in0=y2_tiles[k // ROUND][:, k % ROUND, :], scalar=1.0,
                in1=res[:, k % CHUNK, D_CONTENT:D_MODEL],
                op0=ALU.mult, op1=ALU.add, accum_out=sums[:, 1:2],
            )
            z_tiles[k] = z
            sums_tiles[k] = sums

        def mean(k):
            scaled_sums = stats.tile([P, 2], F32)
            neg_mean = stats.tile([P, 1], F32)
            nc.scalar.activation(
                out=scaled_sums[:], in_=sums_tiles[k][:], func=ACT.Copy, scale=-1.0 / D_MODEL, accum_out=neg_mean[:, 0:1],
            )
            mean_tiles[k] = neg_mean

        def centre_and_gain(k):
            u = upool.tile([P, D_MODEL], F32)
            nc.vector.scalar_tensor_tensor(
                out=u[:], in0=z_tiles[k][:], scalar=mean_tiles[k][:, 0:1], in1=gain[:], op0=ALU.add, op1=ALU.mult,
            )
            u_tiles[k] = u

        def deviation_round(rnd):
            sum_sq = stats.tile([P, ROUND], F32)
            for k in tiles_of(rnd):
                squares = scratch.tile([P, D_MODEL], F32)
                nc.scalar.activation(
                    out=squares[:], in_=z_tiles[k][:], func=ACT.Square, bias=mean_tiles[k][:, 0:1], scale=1.0,
                    accum_out=sum_sq[:, k % ROUND : k % ROUND + 1],
                )
            sigma = stats.tile([P, ROUND], F32)
            nc.scalar.activation(out=sigma[:], in_=sum_sq[:], func=ACT.Sqrt, scale=1.0 / (D_MODEL - 1))
            sigma_eps = stats.tile([P, ROUND], F32)
            nc.scalar.activation(out=sigma_eps[:], in_=sigma[:], func=ACT.Identity, bias=EPS, scale=1.0)
            sigma_tiles[rnd] = sigma_eps

        def invert_round(rnd):
            inv = stats.tile([P, ROUND], F32)
            nc.vector.reciprocal(out=inv[:], in_=sigma_tiles[rnd][:])
            inv_tiles[rnd] = inv

        def finish_round(rnd):
            o = result.tile([P, ROUND, D_MODEL], F32)
            for k in tiles_of(rnd):
                j = k % ROUND
                nc.vector.scalar_tensor_tensor(
                    out=o[:, j, :], in0=u_tiles[k][:], scalar=inv_tiles[rnd][:, j : j + 1], in1=shift[:],
                    op0=ALU.mult, op1=ALU.add,
                )
            k0 = rnd * ROUND
            nc.sync.dma_start(out=out_view[:, k0 : k0 + ROUND, :], in_=o[:])

        def live(rnd):
            return 0 <= rnd < N_ROUNDS

        for step in range(N_ROUNDS + 5):
            if step % ROUNDS_PER_CHUNK == 0:
                c = step // ROUNDS_PER_CHUNK
                if c + CHUNKS_AHEAD < N_CHUNKS:
                    load_x(c + CHUNKS_AHEAD)
                if c < N_CHUNKS:
                    load_residual(c)
            if live(step - 4):
                invert_round(step - 4)
            if live(step - 3):
                for k in tiles_of(step - 3):
                    add_residual(k)
            if live(step):
                transpose_round(step)
            if live(step - 3):
                for k in tiles_of(step - 3):
                    mean(k)
                deviation_round(step - 3)
            if live(step - 4):
                finish_round(step - 4)
            if live(step - 3):
                for k in tiles_of(step - 3):
                    centre_and_gain(k)
            if live(step - 1):
                for k in tiles_of(step - 1):
                    quantise(k)
            if live(step - 2):
                multiply_round(step - 2)
